import numpy as np
import ml_dtypes


def mxq(x, axis, fmt="e4m3"):
    dtype, down = {"e4m3": (ml_dtypes.float8_e4m3fn, 7), "e5m2": (ml_dtypes.float8_e5m2, 14)}[fmt]
    v = np.moveaxis(np.asarray(x, np.float32).astype(ml_dtypes.bfloat16).astype(np.float64), axis, -1)
    blocks = v.reshape(v.shape[:-1] + (-1, 32))
    amax = np.abs(blocks).max(-1, keepdims=True)
    byte = np.maximum(np.where(amax > 0, np.frexp(amax)[1] - 1 + 127, 0) - down, 1)
    scale = np.exp2(byte - 127.0)
    codes = (blocks / scale).astype(np.float32).astype(dtype).astype(np.float64)
    return np.moveaxis((codes * scale).reshape(v.shape), -1, axis)


WIDE = False


def mx_kscale(k):
    if not WIDE:
        return np.ones(k)
    levels = np.array([10, -10, 5, -5, 0])
    a = np.random.permutation(np.resize(levels, k // 512 * 4)).reshape(k // 512, 4)
    idx = np.arange(k)
    return np.exp2(a[idx // 512, idx % 128 // 32])


BF16 = ml_dtypes.bfloat16


def bf(x):
    return np.asarray(x, np.float32).astype(BF16)


def f64(x):
    return np.asarray(x).astype(np.float64)


E2M1 = np.array([0.0, 0.5, 1.0, 1.5, 2.0, 3.0, 4.0, 6.0, -0.0, -0.5, -1.0, -1.5, -2.0, -3.0, -4.0, -6.0])


def pack_weight(w, fmt):
    k, n = w.shape
    w = f64(bf(w)).reshape(k // 32, 32, n)
    amax = np.abs(w).max(1)
    if fmt == "e4m3":
        byte = np.frexp(amax)[1] - 1 + 127 - 7
    else:
        mant, ex = np.frexp(amax / 6.0)
        byte = np.where(mant > 0.5, ex, ex - 1) + 127
    byte = np.clip(np.where(amax > 0, byte, 1), 1, 254)
    scaled = (w * np.exp2(127.0 - byte)[:, None, :]).reshape(k, n).astype(np.float32)
    by_word = np.ascontiguousarray(scaled.reshape(k // 512, 128, 4, n).transpose(0, 1, 3, 2))
    if fmt == "e4m3":
        words = by_word.astype(ml_dtypes.float8_e4m3fn).view(np.uint8)
    else:
        c = by_word.astype(ml_dtypes.float4_e2m1fn).view(np.uint8) & 0xF
        words = c[..., 0::2] | (c[..., 1::2] << 4)
    return np.ascontiguousarray(words), np.ascontiguousarray(byte.astype(np.uint8).reshape(k // 512, 16, n))


def unpack_weight(words, scales, fmt):
    g, p, n, _ = words.shape
    if fmt == "e4m3":
        vals = np.ascontiguousarray(words).view(ml_dtypes.float8_e4m3fn).astype(np.float64)
    else:
        nib = np.empty((g, p, n, 4), np.uint8)
        nib[..., 0::2] = words & 0xF
        nib[..., 1::2] = words >> 4
        vals = E2M1[nib]
    vals = vals * np.repeat(np.exp2(scales.astype(np.float64) - 127.0), 8, axis=1)[..., None]
    return vals.transpose(0, 1, 3, 2).reshape(g * 512, n)


N, DEG, A, B, H = 8, 32, 16384, 512, 512
FMT = "e4m3"


def setup_inputs():
    s, t = mx_kscale(A), mx_kscale(H)
    src_h = bf(np.random.standard_normal((N, DEG, A)) * s)
    he = bf(np.random.standard_normal((N, DEG, B)))
    Wcf_w = np.random.standard_normal((H, A)) / np.sqrt(A) / s[None, :]
    Wcf_b = bf(np.random.standard_normal(H) * 0.3)
    Wdf_w = bf(np.random.standard_normal((H, B)) / np.sqrt(B) * t[:, None])
    Wdf_b = bf(np.random.standard_normal(H) * 0.3 * t)
    Wfc_w = np.random.standard_normal((A, H)) * 0.8 / np.sqrt(H) / t[None, :]
    Wfc_b = bf(np.random.standard_normal(A) * 0.2)
    Wcf_w_words, Wcf_w_scales = pack_weight(np.ascontiguousarray(Wcf_w.T), FMT)
    Wfc_w_words, Wfc_w_scales = pack_weight(np.ascontiguousarray(Wfc_w.T), FMT)
    return {
        "src_h": src_h,
        "he": he,
        "Wcf_w_words": Wcf_w_words,
        "Wcf_w_scales": Wcf_w_scales,
        "Wcf_b": Wcf_b,
        "Wdf_w": Wdf_w,
        "Wdf_b": Wdf_b,
        "Wfc_w_words": Wfc_w_words,
        "Wfc_w_scales": Wfc_w_scales,
        "Wfc_b": Wfc_b,
    }


def reference(src_h, he, Wcf_w_words, Wcf_w_scales, Wcf_b, Wdf_w, Wdf_b, Wfc_w_words, Wfc_w_scales, Wfc_b):
    h_w = (mxq(f64(src_h), 2, "e4m3") @ unpack_weight(Wcf_w_words, Wcf_w_scales, FMT)) + f64(Wcf_b)
    e_vw = f64(he) @ f64(Wdf_w).T + f64(Wdf_b)
    h = h_w * e_vw
    h = (mxq(h, 2, "e4m3") @ unpack_weight(Wfc_w_words, Wfc_w_scales, FMT)) + f64(Wfc_b)
    return np.sum(np.tanh(h), axis=1)

@@ -1,0 +1,301 @@
+from contextlib import ExitStack
+
+import concourse.mybir as mybir
+from concourse.masks import make_identity
+
+F32 = mybir.dt.float32
+BF16 = mybir.dt.bfloat16
+I32 = mybir.dt.int32
+U32 = mybir.dt.uint32
+U8 = mybir.dt.uint8
+FP8X4 = mybir.dt.float8_e4m3fn_x4
+ACT = mybir.ActivationFunctionType
+ALU = mybir.AluOpType
+AXIS = mybir.AxisListType
+
+P = 128
+PACK = 4
+K_PASS = P * PACK
+
+NODES = 8
+DEG = 32
+TOKENS = NODES * DEG
+TOKEN_TILES = TOKENS // P
+ATOMS = 16384
+BOND = 512
+HIDDEN = 512
+
+GROUPS = ATOMS // K_PASS
+ROUND = 4
+ROUNDS = GROUPS // ROUND
+ROUND_ATOMS = ROUND * K_PASS
+
+ATOM_TILES = ATOMS // P
+CHUNK_TILES = 16
+CHUNKS = ATOM_TILES // CHUNK_TILES
+PLANE_TILES = ATOM_TILES // 4
+SUM_TILES = 2
+BLOCK_TILES = P // NODES
+STORE_LAG = 8
+
+FLOPS = 2 * TOKENS * (ATOMS * HIDDEN + BOND * HIDDEN + HIDDEN * ATOMS)
+
+
+def tile_dtnnmsg_k_kernel(
+    tc, src_h, he, Wcf_w_words, Wcf_w_scales, Wcf_b, Wdf_w, Wdf_b, Wfc_w_words, Wfc_w_scales, Wfc_b, out
+):
+    nc = tc.nc
+    src = src_h.flatten_outer_dims()
+    bonds = he.flatten_outer_dims()
+    wcf_words = Wcf_w_words.rearrange("g p n t -> g p (n t)").bitcast(I32)
+    wfc_words = Wfc_w_words.rearrange("g p n t -> (g p) (n t)").bitcast(I32)
+
+    with ExitStack() as stack:
+        const = stack.enter_context(tc.tile_pool(name="const", bufs=1))
+        stream = stack.enter_context(tc.tile_pool(name="stream", bufs=2 * ROUNDS))
+        grouped_pool = stack.enter_context(tc.tile_pool(name="grouped", bufs=2 * ROUND))
+        codes_pool = stack.enter_context(tc.tile_pool(name="codes", bufs=3 * ROUND))
+        tanh_pool = stack.enter_context(tc.tile_pool(name="tanh", bufs=4))
+        store_pool = stack.enter_context(tc.tile_pool(name="store", bufs=2))
+        acc_psum = stack.enter_context(tc.psum_pool(name="acc_psum", bufs=2))
+        bank_psum = stack.enter_context(tc.psum_pool(name="bank_psum", bufs=6))
+        stack.enter_context(tc.manual_schedule())
+
+        wcf_planes = const.tile([P, ROUNDS, HIDDEN], U8, align_bytes=64)
+        wfc_planes = const.tile([P, PLANE_TILES * P], U8, align_bytes=64)
+        nc.vector.memset(wcf_planes[:].rearrange("p r n -> p (r n)").bitcast(I32), 0)
+        nc.vector.memset(wfc_planes[:].bitcast(I32), 0)
+        zero = const.tile([P, 1], F32)
+        nc.vector.memset(zero[:], 0.0)
+
+        ident_bf16 = const.tile([P, P], BF16)
+        make_identity(nc, ident_bf16[:])
+        ident_f32 = const.tile([P, P], F32)
+        make_identity(nc, ident_f32[:])
+
+        bonds_sb = const.tile([P, TOKEN_TILES, BOND], BF16)
+        nc.sync.dma_start(out=bonds_sb[:], in_=bonds.rearrange("(i p) b -> p i b", p=P))
+        wdf_sb = const.tile([P, PACK, BOND], BF16)
+        nc.sync.dma_start(out=wdf_sb[:], in_=Wdf_w.rearrange("(p t) b -> p t b", t=PACK))
+        wdf_bias_bf16 = const.tile([P, PACK], BF16)
+        nc.sync.dma_start(out=wdf_bias_bf16[:], in_=Wdf_b.rearrange("(p t) -> p t", t=PACK))
+        wcf_bias_bf16 = const.tile([P, PACK], BF16)
+        nc.sync.dma_start(out=wcf_bias_bf16[:], in_=Wcf_b.rearrange("(p t) -> p t", t=PACK))
+        wfc_bias_rows = const.tile([P, P], BF16)
+        nc.sync.dma_start(out=wfc_bias_rows[:], in_=Wfc_b.rearrange("(a p) -> a p", p=P))
+
+        warm = const.tile([P, 1], F32)
+        nc.scalar.activation(out=warm[:], in_=zero[:], func=ACT.Tanh)
+
+        def load_wcf_scales(r):
+            for quad in range(4):
+                nc.sync.dma_start(
+                    out=wcf_planes[32 * quad : 32 * quad + 16, r, :].bitcast(I32),
+                    in_=Wcf_w_scales[ROUND * r : ROUND * (r + 1), 4 * quad : 4 * quad + 4, :].bitcast(I32),
+                )
+
+        def load_src(r):
+            piece = stream.tile([P, TOKEN_TILES, ROUND_ATOMS], BF16, tag="piece", align_bytes=64)
+            nc.sync.dma_start(
+                out=piece[:],
+                in_=src[:, ROUND_ATOMS * r : ROUND_ATOMS * (r + 1)].rearrange("(i p) k -> p i k", p=P),
+            )
+            return piece
+
+        def load_wcf(r):
+            piece = stream.tile([P, ROUND, HIDDEN], U32, tag="piece", align_bytes=64)
+            nc.sync.dma_start(
+                out=piece[:].bitcast(I32),
+                in_=wcf_words[ROUND * r : ROUND * (r + 1)].rearrange("g p n -> p g n"),
+            )
+            return piece
+
+        src_pieces = [load_src(0)]
+        wcf_pieces = []
+        for r in range(ROUNDS):
+            load_wcf_scales(r)
+            if r + 1 < ROUNDS:
+                src_pieces.append(load_src(r + 1))
+            wcf_pieces.append(load_wcf(r))
+
+        bonds_ps = bank_psum.tile([P, PACK, TOKEN_TILES, P], BF16, tag="bank")
+        for kb in range(BOND // P):
+            for i in range(TOKEN_TILES):
+                nc.tensor.transpose(bonds_ps[:, kb, i, :], bonds_sb[:, i, P * kb : P * (kb + 1)], ident_bf16[:])
+        bondsT = const.tile([P, BOND // P, TOKENS], BF16)
+        nc.vector.tensor_copy(out=bondsT[:].rearrange("p k c -> p (k c)"), in_=bonds_ps[:].rearrange("p k i c -> p (k i c)"))
+
+        wdfT = const.tile([P, BOND // P, PACK, P], BF16)
+        for half in range(2):
+            wdf_ps = bank_psum.tile([P, 2, PACK, P], BF16, tag="bank")
+            for kl in range(2):
+                kb = 2 * half + kl
+                for t in range(PACK):
+                    nc.tensor.transpose(wdf_ps[:, kl, t, :], wdf_sb[:, t, P * kb : P * (kb + 1)], ident_bf16[:])
+            nc.scalar.copy(
+                out=wdfT[:, 2 * half : 2 * half + 2, :, :].rearrange("p k t j -> p (k t j)"),
+                in_=wdf_ps[:].rearrange("p k t j -> p (k t j)"),
+            )
+
+        wdf_bias = const.tile([P, PACK], F32)
+        nc.vector.tensor_copy(out=wdf_bias[:], in_=wdf_bias_bf16[:])
+
+        e_vwT = const.tile([P, PACK, TOKENS], F32)
+        for half in range(2):
+            e_ps = acc_psum.tile([P, 2, TOKENS], F32, tag="acc")
+            for tl in range(2):
+                t = 2 * half + tl
+                for kb in range(BOND // P):
+                    nc.tensor.matmul(
+                        out=e_ps[:, tl, :],
+                        lhsT=wdfT[:, kb, t, :],
+                        rhs=bondsT[:, kb, :],
+                        start=(kb == 0),
+                        stop=(kb == BOND // P - 1),
+                    )
+            for tl in range(2):
+                t = 2 * half + tl
+                nc.scalar.activation(
+                    out=e_vwT[:, t, :], in_=e_ps[:, tl, :], func=ACT.Identity, bias=wdf_bias[:, t : t + 1]
+                )
+
+        bias_ps = bank_psum.tile([P, PACK, P], F32, tag="bank")
+        for t in range(PACK):
+            nc.tensor.matmul(
+                out=bias_ps[:, t, :],
+                lhsT=wcf_bias_bf16[:, t : t + 1].to_broadcast([P, P]),
+                rhs=ident_bf16[:],
+                start=True,
+                stop=True,
+            )
+        wcf_bias_all = const.tile([P, PACK, P], F32)
+        nc.vector.tensor_copy(out=wcf_bias_all[:], in_=bias_ps[:])
+
+        wfc_bias_ps = bank_psum.tile([P, P], BF16, tag="bank")
+        nc.tensor.transpose(wfc_bias_ps[:], wfc_bias_rows[:], ident_bf16[:])
+        wfc_bias = const.tile([P, P], F32)
+        nc.vector.tensor_copy(out=wfc_bias[:], in_=wfc_bias_ps[:])
+
+        def quantise_group(g):
+            r, j = divmod(g, ROUND)
+            words = src_pieces[r][:].bitcast(F32)
+            pairs_ps = bank_psum.tile([P, 2, TOKENS], F32, tag="bank")
+            for i in range(TOKEN_TILES):
+                for u in range(2):
+                    nc.tensor.transpose(
+                        pairs_ps[:, u, P * i : P * (i + 1)],
+                        words[:, i, 256 * j + u : 256 * (j + 1) : 2],
+                        ident_f32[:],
+                    )
+            grouped = grouped_pool.tile([P, PACK * TOKENS], BF16, align_bytes=64)
+            nc.scalar.copy(
+                out=grouped[:].bitcast(F32).rearrange("p (c u) -> p c u", u=2),
+                in_=pairs_ps[:].rearrange("p u c -> p c u"),
+            )
+            codes = codes_pool.tile([P, TOKENS], U32, align_bytes=64)
+            plane = codes_pool.tile([P, TOKENS], U8, align_bytes=64)
+            nc.vector.quantize_mx(out=codes[:].bitcast(FP8X4), scales=plane[:], in_=grouped[:])
+            return codes, plane
+
+        h_w = [acc_psum.tile([P, HIDDEN], F32, tag="acc", name="h_w%d" % i) for i in range(TOKEN_TILES)]
+
+        def multiply_round(r, quantised):
+            for i in range(TOKEN_TILES):
+                for j in range(ROUND):
+                    g = ROUND * r + j
+                    codes, plane = quantised[j]
+                    nc.tensor.matmul_mx(
+                        out=h_w[i][:],
+                        lhsT=codes[:, P * i : P * (i + 1)].bitcast(FP8X4),
+                        lhsT_scale=plane[:, P * i : P * (i + 1)],
+                        rhs=wcf_pieces[r][:, j, :].bitcast(FP8X4),
+                        rhs_scale=wcf_planes[4 * j : P, r, :],
+                        start=(g == 0),
+                        stop=(g == GROUPS - 1),
+                    )
+
+        ahead = [quantise_group(g) for g in range(ROUND)]
+        for r in range(ROUNDS):
+            now = ahead
+            if r + 1 < ROUNDS:
+                ahead = [quantise_group(ROUND * (r + 1) + j) for j in range(ROUND)]
+            multiply_round(r, now)
+
+        for quad in range(4):
+            nc.sync.dma_start(
+                out=wfc_planes[32 * quad : 32 * quad + 16, :].bitcast(I32),
+                in_=Wfc_w_scales[0, 4 * quad : 4 * quad + 4, :].rearrange("q (j n) -> j q n", j=4).bitcast(I32),
+            )
+        wfc_pieces = []
+        for c in range(CHUNKS):
+            piece = stream.tile([P, CHUNK_TILES * P], U32, tag="piece", align_bytes=64)
+            nc.sync.dma_start(
+                out=piece[:].bitcast(I32), in_=wfc_words[:, CHUNK_TILES * P * c : CHUNK_TILES * P * (c + 1)]
+            )
+            wfc_pieces.append(piece)
+
+        h_grouped = const.tile([P, TOKENS, PACK], BF16, align_bytes=64)
+        h_codes = const.tile([P, TOKENS], U32, align_bytes=64)
+        h_plane = const.tile([P, TOKENS], U8, align_bytes=64)
+        biased = []
+        for i in range(TOKEN_TILES):
+            h_wb = const.tile([P, PACK, P], F32, name="h_wb%d" % i)
+            nc.vector.tensor_tensor(
+                out=h_wb[:], in0=h_w[i][:].rearrange("p (j t) -> p t j", t=PACK), in1=wcf_bias_all[:], op=ALU.add
+            )
+            biased.append(h_wb)
+        for i in range(TOKEN_TILES):
+            tokens = slice(P * i, P * (i + 1))
+            h_wT = acc_psum.tile([P, PACK, P], F32, tag="acc")
+            for t in range(PACK):
+                nc.tensor.transpose(h_wT[:, t, :], biased[i][:, t, :], ident_f32[:])
+            nc.vector.tensor_tensor(
+                out=h_grouped[:, tokens, :],
+                in0=h_wT[:].rearrange("p t c -> p c t"),
+                in1=e_vwT[:, :, tokens].rearrange("p t c -> p c t"),
+                op=ALU.mult,
+            )
+            nc.vector.quantize_mx(
+                out=h_codes[:, tokens].bitcast(FP8X4),
+                scales=h_plane[:, tokens],
+                in_=h_grouped[:, tokens, :].rearrange("p c t -> p (c t)"),
+            )
+
+        sums = const.tile([P, ATOM_TILES * NODES], F32)
+
+        def store_block(b):
+            sums_ps = bank_psum.tile([P, P], F32, tag="bank")
+            nc.tensor.transpose(sums_ps[:], sums[:, P * b : P * (b + 1)], ident_f32[:])
+            rows = store_pool.tile([P, P], F32)
+            nc.vector.tensor_copy(out=rows[:], in_=sums_ps[:])
+            nc.sync.dma_start(
+                out=out[:, BLOCK_TILES * P * b : BLOCK_TILES * P * (b + 1)].rearrange("n (a p) -> a n p", p=P),
+                in_=rows[:],
+            )
+
+        for a in range(ATOM_TILES):
+            cols = slice(P * (a % CHUNK_TILES), P * (a % CHUNK_TILES + 1))
+            plane_cols = slice(P * (a % PLANE_TILES), P * (a % PLANE_TILES + 1))
+            z = bank_psum.tile([P, TOKENS], F32, tag="bank")
+            nc.tensor.matmul_mx(
+                out=z[:],
+                lhsT=wfc_pieces[a // CHUNK_TILES][:, cols].bitcast(FP8X4),
+                lhsT_scale=wfc_planes[4 * (a // PLANE_TILES) : P, plane_cols],
+                rhs=h_codes[:].bitcast(FP8X4),
+                rhs_scale=h_plane[:],
+                start=True,
+                stop=True,
+            )
+            if a % SUM_TILES == 0:
+                tanh_z = tanh_pool.tile([P, SUM_TILES, TOKENS], F32)
+            nc.scalar.activation(out=tanh_z[:, a % SUM_TILES, :], in_=z[:], func=ACT.Tanh, bias=wfc_bias[:, a : a + 1])
+            if a % SUM_TILES == SUM_TILES - 1:
+                nc.vector.tensor_reduce(
+                    out=sums[:, NODES * (a + 1 - SUM_TILES) : NODES * (a + 1)],
+                    in_=tanh_z[:].rearrange("p a (n k) -> p (a n) k", k=DEG),
+                    axis=AXIS.X,
+                    op=ALU.add,
+                )
+            if a >= BLOCK_TILES and a % BLOCK_TILES == STORE_LAG:
+                store_block(a // BLOCK_TILES - 1)
+        store_block(ATOM_TILES // BLOCK_TILES - 1)

@@ -53,6 +53,7 @@ def tile_dtnnmsg_k_kernel(
     with ExitStack() as stack:
         const = stack.enter_context(tc.tile_pool(name="const", bufs=1))
         stream = stack.enter_context(tc.tile_pool(name="stream", bufs=2 * ROUNDS))
+        sorted_pool = stack.enter_context(tc.tile_pool(name="sorted", bufs=2))
         grouped_pool = stack.enter_context(tc.tile_pool(name="grouped", bufs=2 * ROUND))
         codes_pool = stack.enter_context(tc.tile_pool(name="codes", bufs=3 * ROUND))
         tanh_pool = stack.enter_context(tc.tile_pool(name="tanh", bufs=4))
@@ -68,21 +69,16 @@ def tile_dtnnmsg_k_kernel(
         zero = const.tile([P, 1], F32)
         nc.vector.memset(zero[:], 0.0)
 
-        ident_bf16 = const.tile([P, P], BF16)
-        make_identity(nc, ident_bf16[:])
         ident_f32 = const.tile([P, P], F32)
         make_identity(nc, ident_f32[:])
+        ident_bf16 = const.tile([P, P], BF16)
+        make_identity(nc, ident_bf16[:])
 
         bonds_sb = const.tile([P, TOKEN_TILES, BOND], BF16)
-        nc.sync.dma_start(out=bonds_sb[:], in_=bonds.rearrange("(i p) b -> p i b", p=P))
         wdf_sb = const.tile([P, PACK, BOND], BF16)
-        nc.sync.dma_start(out=wdf_sb[:], in_=Wdf_w.rearrange("(p t) b -> p t b", t=PACK))
         wdf_bias_bf16 = const.tile([P, PACK], BF16)
-        nc.sync.dma_start(out=wdf_bias_bf16[:], in_=Wdf_b.rearrange("(p t) -> p t", t=PACK))
         wcf_bias_bf16 = const.tile([P, PACK], BF16)
-        nc.sync.dma_start(out=wcf_bias_bf16[:], in_=Wcf_b.rearrange("(p t) -> p t", t=PACK))
         wfc_bias_rows = const.tile([P, P], BF16)
-        nc.sync.dma_start(out=wfc_bias_rows[:], in_=Wfc_b.rearrange("(a p) -> a p", p=P))
 
         warm = const.tile([P, 1], F32)
         nc.scalar.activation(out=warm[:], in_=zero[:], func=ACT.Tanh)
@@ -96,27 +92,77 @@ def tile_dtnnmsg_k_kernel(
 
         def load_src(r):
             piece = stream.tile([P, TOKEN_TILES, ROUND_ATOMS], BF16, tag="piece", align_bytes=64)
-            nc.sync.dma_start(
-                out=piece[:],
-                in_=src[:, ROUND_ATOMS * r : ROUND_ATOMS * (r + 1)].rearrange("(i p) k -> p i k", p=P),
-            )
+            part = ROUND_ATOMS if r > 0 else ROUND_ATOMS // 2
+            for k in range(0, ROUND_ATOMS, part):
+                nc.sync.dma_start(
+                    out=piece[:, :, k : k + part],
+                    in_=src[:, ROUND_ATOMS * r + k : ROUND_ATOMS * r + k + part].rearrange("(i p) k -> p i k", p=P),
+                )
             return piece
 
         def load_wcf(r):
             piece = stream.tile([P, ROUND, HIDDEN], U32, tag="piece", align_bytes=64)
-            nc.sync.dma_start(
-                out=piece[:].bitcast(I32),
-                in_=wcf_words[ROUND * r : ROUND * (r + 1)].rearrange("g p n -> p g n"),
-            )
+            part = ROUND if r + 1 < ROUNDS else 1
+            for j in range(0, ROUND, part):
+                nc.sync.dma_start(
+                    out=piece[:, j : j + part, :].bitcast(I32),
+                    in_=wcf_words[ROUND * r + j : ROUND * r + j + part].rearrange("g p n -> p g n"),
+                )
             return piece
 
         src_pieces = [load_src(0)]
+        nc.sync.dma_start(out=bonds_sb[:], in_=bonds.rearrange("(i p) b -> p i b", p=P))
+        nc.sync.dma_start(out=wdf_sb[:], in_=Wdf_w.rearrange("(p t) b -> p t b", t=PACK))
         wcf_pieces = []
         for r in range(ROUNDS):
-            load_wcf_scales(r)
             if r + 1 < ROUNDS:
                 src_pieces.append(load_src(r + 1))
+            load_wcf_scales(r)
             wcf_pieces.append(load_wcf(r))
+            if r == 0:
+                nc.sync.dma_start(out=wdf_bias_bf16[:], in_=Wdf_b.rearrange("(p t) -> p t", t=PACK))
+                nc.sync.dma_start(out=wcf_bias_bf16[:], in_=Wcf_b.rearrange("(p t) -> p t", t=PACK))
+                nc.sync.dma_start(out=wfc_bias_rows[:], in_=Wfc_b.rearrange("(a p) -> a p", p=P))
+
+        sorted_words = []
+
+        def sort_piece(r):
+            words = src_pieces[r][:].bitcast(F32)
+            by_u = sorted_pool.tile([P, TOKEN_TILES, 2, ROUND * P], F32, name="by_u")
+            half = ROUND * P // 2
+            for k in range(2):
+                nc.vector.tensor_copy(
+                    out=by_u[:, :, :, half * k : half * (k + 1)],
+                    in_=words[:, :, 2 * half * k : 2 * half * (k + 1)].rearrange("p i (w u) -> p i u w", u=2),
+                )
+            sorted_words.append(by_u)
+
+        def transpose_group(g):
+            r, j = divmod(g, ROUND)
+            pairs_ps = bank_psum.tile([P, 2, TOKENS], F32, tag="bank")
+            for i in range(TOKEN_TILES):
+                for u in range(2):
+                    nc.tensor.transpose(
+                        pairs_ps[:, u, P * i : P * (i + 1)],
+                        sorted_words[r][:, i, u, P * j : P * (j + 1)],
+                        ident_f32[:],
+                    )
+            grouped = grouped_pool.tile([P, PACK * TOKENS], BF16, align_bytes=64)
+            nc.scalar.copy(
+                out=grouped[:].bitcast(F32).rearrange("p (c u) -> p c u", u=2),
+                in_=pairs_ps[:].rearrange("p u c -> p c u"),
+            )
+            return grouped
+
+        def quantise(grouped):
+            codes = codes_pool.tile([P, TOKENS], U32, align_bytes=64)
+            plane = codes_pool.tile([P, TOKENS], U8, align_bytes=64)
+            nc.vector.quantize_mx(out=codes[:].bitcast(FP8X4), scales=plane[:], in_=grouped[:])
+            return codes, plane
+
+        sort_piece(0)
+        grouped = [transpose_group(g) for g in range(ROUND)]
+        ahead = [quantise(x) for x in grouped]
 
         bonds_ps = bank_psum.tile([P, PACK, TOKEN_TILES, P], BF16, tag="bank")
         for kb in range(BOND // P):
@@ -132,76 +178,58 @@ def tile_dtnnmsg_k_kernel(
                 kb = 2 * half + kl
                 for t in range(PACK):
                     nc.tensor.transpose(wdf_ps[:, kl, t, :], wdf_sb[:, t, P * kb : P * (kb + 1)], ident_bf16[:])
-            nc.scalar.copy(
+            (nc.scalar.copy, nc.vector.tensor_copy)[half](
                 out=wdfT[:, 2 * half : 2 * half + 2, :, :].rearrange("p k t j -> p (k t j)"),
                 in_=wdf_ps[:].rearrange("p k t j -> p (k t j)"),
             )
 
-        wdf_bias = const.tile([P, PACK], F32)
-        nc.vector.tensor_copy(out=wdf_bias[:], in_=wdf_bias_bf16[:])
-
-        e_vwT = const.tile([P, PACK, TOKENS], F32)
+        sort_piece(1)
+        e_sums = []
         for half in range(2):
-            e_ps = acc_psum.tile([P, 2, TOKENS], F32, tag="acc")
+            e_ps = bank_psum.tile([P, 2, TOKENS], F32, tag="bank", name="e_ps%d" % half)
             for tl in range(2):
-                t = 2 * half + tl
                 for kb in range(BOND // P):
                     nc.tensor.matmul(
                         out=e_ps[:, tl, :],
-                        lhsT=wdfT[:, kb, t, :],
+                        lhsT=wdfT[:, kb, 2 * half + tl, :],
                         rhs=bondsT[:, kb, :],
                         start=(kb == 0),
                         stop=(kb == BOND // P - 1),
                     )
-            for tl in range(2):
-                t = 2 * half + tl
+            e_sums.append(e_ps)
+
+        e_vwT = const.tile([P, PACK, TOKENS], F32)
+        wcf_bias_all = const.tile([P, PACK, P], F32)
+        wfc_bias = const.tile([P, P], F32)
+
+        def finish_e_vw():
+            wdf_bias = const.tile([P, PACK], F32)
+            nc.vector.tensor_copy(out=wdf_bias[:], in_=wdf_bias_bf16[:])
+            for t in range(PACK):
                 nc.scalar.activation(
-                    out=e_vwT[:, t, :], in_=e_ps[:, tl, :], func=ACT.Identity, bias=wdf_bias[:, t : t + 1]
+                    out=e_vwT[:, t, :], in_=e_sums[t // 2][:, t % 2, :], func=ACT.Identity, bias=wdf_bias[:, t : t + 1]
                 )
 
-        bias_ps = bank_psum.tile([P, PACK, P], F32, tag="bank")
-        for t in range(PACK):
-            nc.tensor.matmul(
-                out=bias_ps[:, t, :],
-                lhsT=wcf_bias_bf16[:, t : t + 1].to_broadcast([P, P]),
-                rhs=ident_bf16[:],
-                start=True,
-                stop=True,
-            )
-        wcf_bias_all = const.tile([P, PACK, P], F32)
-        nc.vector.tensor_copy(out=wcf_bias_all[:], in_=bias_ps[:])
-
-        wfc_bias_ps = bank_psum.tile([P, P], BF16, tag="bank")
-        nc.tensor.transpose(wfc_bias_ps[:], wfc_bias_rows[:], ident_bf16[:])
-        wfc_bias = const.tile([P, P], F32)
-        nc.vector.tensor_copy(out=wfc_bias[:], in_=wfc_bias_ps[:])
-
-        def quantise_group(g):
-            r, j = divmod(g, ROUND)
-            words = src_pieces[r][:].bitcast(F32)
-            pairs_ps = bank_psum.tile([P, 2, TOKENS], F32, tag="bank")
-            for i in range(TOKEN_TILES):
-                for u in range(2):
-                    nc.tensor.transpose(
-                        pairs_ps[:, u, P * i : P * (i + 1)],
-                        words[:, i, 256 * j + u : 256 * (j + 1) : 2],
-                        ident_f32[:],
-                    )
-            grouped = grouped_pool.tile([P, PACK * TOKENS], BF16, align_bytes=64)
-            nc.scalar.copy(
-                out=grouped[:].bitcast(F32).rearrange("p (c u) -> p c u", u=2),
-                in_=pairs_ps[:].rearrange("p u c -> p c u"),
-            )
-            codes = codes_pool.tile([P, TOKENS], U32, align_bytes=64)
-            plane = codes_pool.tile([P, TOKENS], U8, align_bytes=64)
-            nc.vector.quantize_mx(out=codes[:].bitcast(FP8X4), scales=plane[:], in_=grouped[:])
-            return codes, plane
+        def spread_biases():
+            bias_ps = bank_psum.tile([P, PACK, P], F32, tag="bank")
+            for t in range(PACK):
+                nc.tensor.matmul(
+                    out=bias_ps[:, t, :],
+                    lhsT=wcf_bias_bf16[:, t : t + 1].to_broadcast([P, P]),
+                    rhs=ident_bf16[:],
+                    start=True,
+                    stop=True,
+                )
+            nc.vector.tensor_copy(out=wcf_bias_all[:], in_=bias_ps[:])
+            wfc_bias_ps = bank_psum.tile([P, P], BF16, tag="bank")
+            nc.tensor.transpose(wfc_bias_ps[:], wfc_bias_rows[:], ident_bf16[:])
+            nc.vector.tensor_copy(out=wfc_bias[:], in_=wfc_bias_ps[:])
 
         h_w = [acc_psum.tile([P, HIDDEN], F32, tag="acc", name="h_w%d" % i) for i in range(TOKEN_TILES)]
 
         def multiply_round(r, quantised):
-            for i in range(TOKEN_TILES):
-                for j in range(ROUND):
+            for j in range(ROUND):
+                for i in range(TOKEN_TILES):
                     g = ROUND * r + j
                     codes, plane = quantised[j]
                     nc.tensor.matmul_mx(
@@ -214,12 +242,19 @@ def tile_dtnnmsg_k_kernel(
                         stop=(g == GROUPS - 1),
                     )
 
-        ahead = [quantise_group(g) for g in range(ROUND)]
         for r in range(ROUNDS):
             now = ahead
             if r + 1 < ROUNDS:
-                ahead = [quantise_group(ROUND * (r + 1) + j) for j in range(ROUND)]
+                grouped = [transpose_group(ROUND * (r + 1) + j) for j in range(ROUND)]
+                ahead = [quantise(x) for x in grouped[:2]]
+                if r + 2 < ROUNDS:
+                    sort_piece(r + 2)
+                ahead += [quantise(x) for x in grouped[2:]]
+            if r == 0:
+                finish_e_vw()
             multiply_round(r, now)
+            if r == 1:
+                spread_biases()
 
         for quad in range(4):
             nc.sync.dma_start(
@@ -255,11 +290,9 @@ def tile_dtnnmsg_k_kernel(
                 in1=e_vwT[:, :, tokens].rearrange("p t c -> p c t"),
                 op=ALU.mult,
             )
-            nc.vector.quantize_mx(
-                out=h_codes[:, tokens].bitcast(FP8X4),
-                scales=h_plane[:, tokens],
-                in_=h_grouped[:, tokens, :].rearrange("p c t -> p (c t)"),
-            )
+        nc.vector.quantize_mx(
+            out=h_codes[:].bitcast(FP8X4), scales=h_plane[:], in_=h_grouped[:].rearrange("p c t -> p (c t)")
+        )
 
         sums = const.tile([P, ATOM_TILES * NODES], F32)
 

@@ -29,6 +29,9 @@ GROUPS = ATOMS // K_PASS
 ROUND = 4
 ROUNDS = GROUPS // ROUND
 ROUND_ATOMS = ROUND * K_PASS
+STEP = 2
+STEPS = GROUPS // STEP
+AHEAD = 2
 
 ATOM_TILES = ATOMS // P
 CHUNK_TILES = 16
@@ -53,7 +56,7 @@ def tile_dtnnmsg_k_kernel(
     with ExitStack() as stack:
         const = stack.enter_context(tc.tile_pool(name="const", bufs=1))
         stream = stack.enter_context(tc.tile_pool(name="stream", bufs=2 * ROUNDS))
-        sorted_pool = stack.enter_context(tc.tile_pool(name="sorted", bufs=2))
+        sorted_pool = stack.enter_context(tc.tile_pool(name="sorted", bufs=4))
         grouped_pool = stack.enter_context(tc.tile_pool(name="grouped", bufs=2 * ROUND))
         codes_pool = stack.enter_context(tc.tile_pool(name="codes", bufs=3 * ROUND))
         tanh_pool = stack.enter_context(tc.tile_pool(name="tanh", bufs=4))
@@ -126,25 +129,23 @@ def tile_dtnnmsg_k_kernel(
 
         sorted_words = []
 
-        def sort_piece(r):
-            words = src_pieces[r][:].bitcast(F32)
-            by_u = sorted_pool.tile([P, TOKEN_TILES, 2, ROUND * P], F32, name="by_u")
-            half = ROUND * P // 2
-            for k in range(2):
-                nc.vector.tensor_copy(
-                    out=by_u[:, :, :, half * k : half * (k + 1)],
-                    in_=words[:, :, 2 * half * k : 2 * half * (k + 1)].rearrange("p i (w u) -> p i u w", u=2),
-                )
+        def sort_step(k):
+            words = src_pieces[k * STEP // ROUND][:].bitcast(F32)
+            first = 2 * P * (k * STEP % ROUND)
+            by_u = sorted_pool.tile([P, TOKEN_TILES, 2, STEP * P], F32, name="by_u")
+            nc.vector.tensor_copy(
+                out=by_u[:], in_=words[:, :, first : first + 2 * P * STEP].rearrange("p i (w u) -> p i u w", u=2)
+            )
             sorted_words.append(by_u)
 
         def transpose_group(g):
-            r, j = divmod(g, ROUND)
+            k, j = divmod(g, STEP)
             pairs_ps = bank_psum.tile([P, 2, TOKENS], F32, tag="bank")
             for i in range(TOKEN_TILES):
                 for u in range(2):
                     nc.tensor.transpose(
                         pairs_ps[:, u, P * i : P * (i + 1)],
-                        sorted_words[r][:, i, u, P * j : P * (j + 1)],
+                        sorted_words[k][:, i, u, P * j : P * (j + 1)],
                         ident_f32[:],
                     )
             grouped = grouped_pool.tile([P, PACK * TOKENS], BF16, align_bytes=64)
@@ -160,9 +161,14 @@ def tile_dtnnmsg_k_kernel(
             nc.vector.quantize_mx(out=codes[:].bitcast(FP8X4), scales=plane[:], in_=grouped[:])
             return codes, plane
 
-        sort_piece(0)
-        grouped = [transpose_group(g) for g in range(ROUND)]
-        ahead = [quantise(x) for x in grouped]
+        def transpose_step(k):
+            return [transpose_group(STEP * k + j) for j in range(STEP)]
+
+        quantised = []
+        for k in range(AHEAD):
+            sort_step(k)
+            grouped = transpose_step(k)
+            quantised.append([quantise(x) for x in grouped])
 
         bonds_ps = bank_psum.tile([P, PACK, TOKEN_TILES, P], BF16, tag="bank")
         for kb in range(BOND // P):
@@ -183,7 +189,7 @@ def tile_dtnnmsg_k_kernel(
                 in_=wdf_ps[:].rearrange("p k t j -> p (k t j)"),
             )
 
-        sort_piece(1)
+        sort_step(AHEAD)
         e_sums = []
         for half in range(2):
             e_ps = bank_psum.tile([P, 2, TOKENS], F32, tag="bank", name="e_ps%d" % half)
@@ -227,11 +233,11 @@ def tile_dtnnmsg_k_kernel(
 
         h_w = [acc_psum.tile([P, HIDDEN], F32, tag="acc", name="h_w%d" % i) for i in range(TOKEN_TILES)]
 
-        def multiply_round(r, quantised):
-            for j in range(ROUND):
+        def multiply_step(k):
+            for g in range(STEP * k, STEP * (k + 1)):
+                r, j = divmod(g, ROUND)
+                codes, plane = quantised[k][g % STEP]
                 for i in range(TOKEN_TILES):
-                    g = ROUND * r + j
-                    codes, plane = quantised[j]
                     nc.tensor.matmul_mx(
                         out=h_w[i][:],
                         lhsT=codes[:, P * i : P * (i + 1)].bitcast(FP8X4),
@@ -242,18 +248,16 @@ def tile_dtnnmsg_k_kernel(
                         stop=(g == GROUPS - 1),
                     )
 
-        for r in range(ROUNDS):
-            now = ahead
-            if r + 1 < ROUNDS:
-                grouped = [transpose_group(ROUND * (r + 1) + j) for j in range(ROUND)]
-                ahead = [quantise(x) for x in grouped[:2]]
-                if r + 2 < ROUNDS:
-                    sort_piece(r + 2)
-                ahead += [quantise(x) for x in grouped[2:]]
-            if r == 0:
+        for k in range(STEPS):
+            if k + AHEAD < STEPS:
+                grouped = transpose_step(k + AHEAD)
+                if k + AHEAD + 1 < STEPS:
+                    sort_step(k + AHEAD + 1)
+                quantised.append([quantise(x) for x in grouped])
+            if k == 1:
                 finish_e_vw()
-            multiply_round(r, now)
-            if r == 1:
+            multiply_step(k)
+            if k == 3:
                 spread_biases()
 
         for quad in range(4):

@@ -164,11 +164,10 @@ def tile_dtnnmsg_k_kernel(
         def transpose_step(k):
             return [transpose_group(STEP * k + j) for j in range(STEP)]
 
-        quantised = []
         for k in range(AHEAD):
             sort_step(k)
-            grouped = transpose_step(k)
-            quantised.append([quantise(x) for x in grouped])
+        grouped = [transpose_step(k) for k in range(AHEAD)]
+        quantised = [[quantise(x) for x in step] for step in grouped]
 
         bonds_ps = bank_psum.tile([P, PACK, TOKEN_TILES, P], BF16, tag="bank")
         for kb in range(BOND // P):
@@ -279,13 +278,17 @@ def tile_dtnnmsg_k_kernel(
         biased = []
         for i in range(TOKEN_TILES):
             h_wb = const.tile([P, PACK, P], F32, name="h_wb%d" % i)
-            nc.vector.tensor_tensor(
-                out=h_wb[:], in0=h_w[i][:].rearrange("p (j t) -> p t j", t=PACK), in1=wcf_bias_all[:], op=ALU.add
-            )
+            for t in range(0, PACK, 2):
+                nc.vector.tensor_tensor(
+                    out=h_wb[:, t : t + 2, :],
+                    in0=h_w[i][:].rearrange("p (j t) -> p t j", t=PACK)[:, t : t + 2, :],
+                    in1=wcf_bias_all[:, t : t + 2, :],
+                    op=ALU.add,
+                )
             biased.append(h_wb)
         for i in range(TOKEN_TILES):
             tokens = slice(P * i, P * (i + 1))
-            h_wT = acc_psum.tile([P, PACK, P], F32, tag="acc")
+            h_wT = bank_psum.tile([P, PACK, P], F32, tag="bank")
             for t in range(PACK):
                 nc.tensor.transpose(h_wT[:, t, :], biased[i][:, t, :], ident_f32[:])
             nc.vector.tensor_tensor(
@@ -294,9 +297,13 @@ def tile_dtnnmsg_k_kernel(
                 in1=e_vwT[:, :, tokens].rearrange("p t c -> p c t"),
                 op=ALU.mult,
             )
-        nc.vector.quantize_mx(
-            out=h_codes[:].bitcast(FP8X4), scales=h_plane[:], in_=h_grouped[:].rearrange("p c t -> p (c t)")
-        )
+        for i in range(TOKEN_TILES):
+            tokens = slice(P * i, P * (i + 1))
+            nc.vector.quantize_mx(
+                out=h_codes[:, tokens].bitcast(FP8X4),
+                scales=h_plane[:, tokens],
+                in_=h_grouped[:, tokens, :].rearrange("p c t -> p (c t)"),
+            )
 
         sums = const.tile([P, ATOM_TILES * NODES], F32)
 

@@ -36,6 +36,7 @@ AHEAD = 2
 ATOM_TILES = ATOMS // P
 CHUNK_TILES = 16
 CHUNKS = ATOM_TILES // CHUNK_TILES
+FIRST_TILES = 4
 PLANE_TILES = ATOM_TILES // 4
 SUM_TILES = 2
 BLOCK_TILES = P // NODES
@@ -67,8 +68,8 @@ def tile_dtnnmsg_k_kernel(
 
         wcf_planes = const.tile([P, ROUNDS, HIDDEN], U8, align_bytes=64)
         wfc_planes = const.tile([P, PLANE_TILES * P], U8, align_bytes=64)
+        wfc_first = const.tile([P, PLANE_TILES * P], U8, align_bytes=64)
         nc.vector.memset(wcf_planes[:].rearrange("p r n -> p (r n)").bitcast(I32), 0)
-        nc.vector.memset(wfc_planes[:].bitcast(I32), 0)
         zero = const.tile([P, 1], F32)
         nc.vector.memset(zero[:], 0.0)
 
@@ -189,6 +190,8 @@ def tile_dtnnmsg_k_kernel(
             )
 
         sort_step(AHEAD)
+        nc.vector.memset(wfc_first[:].bitcast(I32), 0)
+        nc.vector.memset(wfc_planes[:].bitcast(I32), 0)
         e_sums = []
         for half in range(2):
             e_ps = bank_psum.tile([P, 2, TOKENS], F32, tag="bank", name="e_ps%d" % half)
@@ -261,15 +264,24 @@ def tile_dtnnmsg_k_kernel(
 
         for quad in range(4):
             nc.sync.dma_start(
-                out=wfc_planes[32 * quad : 32 * quad + 16, :].bitcast(I32),
-                in_=Wfc_w_scales[0, 4 * quad : 4 * quad + 4, :].rearrange("q (j n) -> j q n", j=4).bitcast(I32),
+                out=wfc_first[32 * quad : 32 * quad + 4, :].bitcast(I32),
+                in_=Wfc_w_scales[0, 4 * quad : 4 * quad + 4, 0 : PLANE_TILES * P].bitcast(I32),
             )
         wfc_pieces = []
         for c in range(CHUNKS):
+            if c == 1:
+                for quad in range(4):
+                    nc.sync.dma_start(
+                        out=wfc_planes[32 * quad : 32 * quad + 16, :].bitcast(I32),
+                        in_=Wfc_w_scales[0, 4 * quad : 4 * quad + 4, :].rearrange("q (j n) -> j q n", j=4).bitcast(I32),
+                    )
             piece = stream.tile([P, CHUNK_TILES * P], U32, tag="piece", align_bytes=64)
-            nc.sync.dma_start(
-                out=piece[:].bitcast(I32), in_=wfc_words[:, CHUNK_TILES * P * c : CHUNK_TILES * P * (c + 1)]
-            )
+            parts = [(0, CHUNK_TILES * P)] if c > 0 else [(0, FIRST_TILES * P), (FIRST_TILES * P, CHUNK_TILES * P)]
+            for start, end in parts:
+                nc.sync.dma_start(
+                    out=piece[:, start:end].bitcast(I32),
+                    in_=wfc_words[:, CHUNK_TILES * P * c + start : CHUNK_TILES * P * c + end],
+                )
             wfc_pieces.append(piece)
 
         h_grouped = const.tile([P, TOKENS, PACK], BF16, align_bytes=64)
@@ -324,7 +336,9 @@ def tile_dtnnmsg_k_kernel(
             nc.tensor.matmul_mx(
                 out=z[:],
                 lhsT=wfc_pieces[a // CHUNK_TILES][:, cols].bitcast(FP8X4),
-                lhsT_scale=wfc_planes[4 * (a // PLANE_TILES) : P, plane_cols],
+                lhsT_scale=wfc_first[:, plane_cols]
+                if a < PLANE_TILES
+                else wfc_planes[4 * (a // PLANE_TILES) : P, plane_cols],
                 rhs=h_codes[:].bitcast(FP8X4),
                 rhs_scale=h_plane[:],
                 start=True,
@@ -333,10 +347,13 @@ def tile_dtnnmsg_k_kernel(
             if a % SUM_TILES == 0:
                 tanh_z = tanh_pool.tile([P, SUM_TILES, TOKENS], F32)
             nc.scalar.activation(out=tanh_z[:, a % SUM_TILES, :], in_=z[:], func=ACT.Tanh, bias=wfc_bias[:, a : a + 1])
-            if a % SUM_TILES == SUM_TILES - 1:
+            width = SUM_TILES if a < ATOM_TILES - SUM_TILES else 1
+            if (a + 1) % width == 0:
                 nc.vector.tensor_reduce(
-                    out=sums[:, NODES * (a + 1 - SUM_TILES) : NODES * (a + 1)],
-                    in_=tanh_z[:].rearrange("p a (n k) -> p (a n) k", k=DEG),
+                    out=sums[:, NODES * (a + 1 - width) : NODES * (a + 1)],
+                    in_=tanh_z[:, (a + 1 - width) % SUM_TILES : a % SUM_TILES + 1, :].rearrange(
+                        "p a (n k) -> p (a n) k", k=DEG
+                    ),
                     axis=AXIS.X,
                     op=ALU.add,
                 )

from contextlib import ExitStack

import concourse.mybir as mybir
from concourse.masks import make_identity

F32 = mybir.dt.float32
BF16 = mybir.dt.bfloat16
I32 = mybir.dt.int32
U32 = mybir.dt.uint32
U8 = mybir.dt.uint8
FP8X4 = mybir.dt.float8_e4m3fn_x4
ACT = mybir.ActivationFunctionType
ALU = mybir.AluOpType
AXIS = mybir.AxisListType

P = 128
PACK = 4
K_PASS = P * PACK

NODES = 8
DEG = 32
TOKENS = NODES * DEG
TOKEN_TILES = TOKENS // P
ATOMS = 16384
BOND = 512
HIDDEN = 512

GROUPS = ATOMS // K_PASS
ROUND = 4
ROUNDS = GROUPS // ROUND
ROUND_ATOMS = ROUND * K_PASS
STEP = 2
STEPS = GROUPS // STEP
AHEAD = 2

ATOM_TILES = ATOMS // P
CHUNK_TILES = 16
CHUNKS = ATOM_TILES // CHUNK_TILES
FIRST_TILES = 4
PLANE_TILES = ATOM_TILES // 4
SUM_TILES = 2
BLOCK_TILES = P // NODES
STORE_LAG = 8

FLOPS = 2 * TOKENS * (ATOMS * HIDDEN + BOND * HIDDEN + HIDDEN * ATOMS)


def tile_dtnnmsg_k_kernel(
    tc, src_h, he, Wcf_w_words, Wcf_w_scales, Wcf_b, Wdf_w, Wdf_b, Wfc_w_words, Wfc_w_scales, Wfc_b, out
):
    nc = tc.nc
    src = src_h.flatten_outer_dims()
    bonds = he.flatten_outer_dims()
    wcf_words = Wcf_w_words.rearrange("g p n t -> g p (n t)").bitcast(I32)
    wfc_words = Wfc_w_words.rearrange("g p n t -> (g p) (n t)").bitcast(I32)

    with ExitStack() as stack:
        const = stack.enter_context(tc.tile_pool(name="const", bufs=1))
        stream = stack.enter_context(tc.tile_pool(name="stream", bufs=2 * ROUNDS))
        sorted_pool = stack.enter_context(tc.tile_pool(name="sorted", bufs=4))
        grouped_pool = stack.enter_context(tc.tile_pool(name="grouped", bufs=2 * ROUND))
        codes_pool = stack.enter_context(tc.tile_pool(name="codes", bufs=3 * ROUND))
        tanh_pool = stack.enter_context(tc.tile_pool(name="tanh", bufs=4))
        store_pool = stack.enter_context(tc.tile_pool(name="store", bufs=2))
        acc_psum = stack.enter_context(tc.psum_pool(name="acc_psum", bufs=2))
        bank_psum = stack.enter_context(tc.psum_pool(name="bank_psum", bufs=6))
        stack.enter_context(tc.manual_schedule())

        wcf_planes = const.tile([P, ROUNDS, HIDDEN], U8, align_bytes=64)
        wfc_planes = const.tile([P, PLANE_TILES * P], U8, align_bytes=64)
        wfc_first = const.tile([P, PLANE_TILES * P], U8, align_bytes=64)
        nc.vector.memset(wcf_planes[:].rearrange("p r n -> p (r n)").bitcast(I32), 0)
        zero = const.tile([P, 1], F32)
        nc.vector.memset(zero[:], 0.0)

        ident_f32 = const.tile([P, P], F32)
        make_identity(nc, ident_f32[:])
        ident_bf16 = const.tile([P, P], BF16)
        make_identity(nc, ident_bf16[:])

        bonds_sb = const.tile([P, TOKEN_TILES, BOND], BF16)
        wdf_sb = const.tile([P, PACK, BOND], BF16)
        wdf_bias_bf16 = const.tile([P, PACK], BF16)
        wcf_bias_bf16 = const.tile([P, PACK], BF16)
        wfc_bias_rows = const.tile([P, P], BF16)

        warm = const.tile([P, 1], F32)
        nc.scalar.activation(out=warm[:], in_=zero[:], func=ACT.Tanh)

        def load_wcf_scales(r):
            for quad in range(4):
                nc.sync.dma_start(
                    out=wcf_planes[32 * quad : 32 * quad + 16, r, :].bitcast(I32),
                    in_=Wcf_w_scales[ROUND * r : ROUND * (r + 1), 4 * quad : 4 * quad + 4, :].bitcast(I32),
                )

        def load_src(r):
            piece = stream.tile([P, TOKEN_TILES, ROUND_ATOMS], BF16, tag="piece", align_bytes=64)
            part = ROUND_ATOMS if r > 0 else ROUND_ATOMS // 2
            for k in range(0, ROUND_ATOMS, part):
                nc.sync.dma_start(
                    out=piece[:, :, k : k + part],
                    in_=src[:, ROUND_ATOMS * r + k : ROUND_ATOMS * r + k + part].rearrange("(i p) k -> p i k", p=P),
                )
            return piece

        def load_wcf(r):
            piece = stream.tile([P, ROUND, HIDDEN], U32, tag="piece", align_bytes=64)
            part = ROUND if r + 1 < ROUNDS else 1
            for j in range(0, ROUND, part):
                nc.sync.dma_start(
                    out=piece[:, j : j + part, :].bitcast(I32),
                    in_=wcf_words[ROUND * r + j : ROUND * r + j + part].rearrange("g p n -> p g n"),
                )
            return piece

        src_pieces = [load_src(0)]
        nc.sync.dma_start(out=bonds_sb[:], in_=bonds.rearrange("(i p) b -> p i b", p=P))
        nc.sync.dma_start(out=wdf_sb[:], in_=Wdf_w.rearrange("(p t) b -> p t b", t=PACK))
        wcf_pieces = []
        for r in range(ROUNDS):
            if r + 1 < ROUNDS:
                src_pieces.append(load_src(r + 1))
            load_wcf_scales(r)
            wcf_pieces.append(load_wcf(r))
            if r == 0:
                nc.sync.dma_start(out=wdf_bias_bf16[:], in_=Wdf_b.rearrange("(p t) -> p t", t=PACK))
                nc.sync.dma_start(out=wcf_bias_bf16[:], in_=Wcf_b.rearrange("(p t) -> p t", t=PACK))
                nc.sync.dma_start(out=wfc_bias_rows[:], in_=Wfc_b.rearrange("(a p) -> a p", p=P))

        sorted_words = []

        def sort_step(k):
            words = src_pieces[k * STEP // ROUND][:].bitcast(F32)
            first = 2 * P * (k * STEP % ROUND)
            by_u = sorted_pool.tile([P, TOKEN_TILES, 2, STEP * P], F32, name="by_u")
            nc.vector.tensor_copy(
                out=by_u[:], in_=words[:, :, first : first + 2 * P * STEP].rearrange("p i (w u) -> p i u w", u=2)
            )
            sorted_words.append(by_u)

        def transpose_group(g):
            k, j = divmod(g, STEP)
            pairs_ps = bank_psum.tile([P, 2, TOKENS], F32, tag="bank")
            for i in range(TOKEN_TILES):
                for u in range(2):
                    nc.tensor.transpose(
                        pairs_ps[:, u, P * i : P * (i + 1)],
                        sorted_words[k][:, i, u, P * j : P * (j + 1)],
                        ident_f32[:],
                    )
            grouped = grouped_pool.tile([P, PACK * TOKENS], BF16, align_bytes=64)
            nc.scalar.copy(
                out=grouped[:].bitcast(F32).rearrange("p (c u) -> p c u", u=2),
                in_=pairs_ps[:].rearrange("p u c -> p c u"),
            )
            return grouped

        def quantise(grouped):
            codes = codes_pool.tile([P, TOKENS], U32, align_bytes=64)
            plane = codes_pool.tile([P, TOKENS], U8, align_bytes=64)
            nc.vector.quantize_mx(out=codes[:].bitcast(FP8X4), scales=plane[:], in_=grouped[:])
            return codes, plane

        def transpose_step(k):
            return [transpose_group(STEP * k + j) for j in range(STEP)]

        for k in range(AHEAD):
            sort_step(k)
        grouped = [transpose_step(k) for k in range(AHEAD)]
        quantised = [[quantise(x) for x in step] for step in grouped]

        bonds_ps = bank_psum.tile([P, PACK, TOKEN_TILES, P], BF16, tag="bank")
        for kb in range(BOND // P):
            for i in range(TOKEN_TILES):
                nc.tensor.transpose(bonds_ps[:, kb, i, :], bonds_sb[:, i, P * kb : P * (kb + 1)], ident_bf16[:])
        bondsT = const.tile([P, BOND // P, TOKENS], BF16)
        nc.vector.tensor_copy(out=bondsT[:].rearrange("p k c -> p (k c)"), in_=bonds_ps[:].rearrange("p k i c -> p (k i c)"))

        wdfT = const.tile([P, BOND // P, PACK, P], BF16)
        for half in range(2):
            wdf_ps = bank_psum.tile([P, 2, PACK, P], BF16, tag="bank")
            for kl in range(2):
                kb = 2 * half + kl
                for t in range(PACK):
                    nc.tensor.transpose(wdf_ps[:, kl, t, :], wdf_sb[:, t, P * kb : P * (kb + 1)], ident_bf16[:])
            (nc.scalar.copy, nc.vector.tensor_copy)[half](
                out=wdfT[:, 2 * half : 2 * half + 2, :, :].rearrange("p k t j -> p (k t j)"),
                in_=wdf_ps[:].rearrange("p k t j -> p (k t j)"),
            )

        sort_step(AHEAD)
        nc.vector.memset(wfc_first[:].bitcast(I32), 0)
        nc.vector.memset(wfc_planes[:].bitcast(I32), 0)
        e_sums = []
        for half in range(2):
            e_ps = bank_psum.tile([P, 2, TOKENS], F32, tag="bank", name="e_ps%d" % half)
            for tl in range(2):
                for kb in range(BOND // P):
                    nc.tensor.matmul(
                        out=e_ps[:, tl, :],
                        lhsT=wdfT[:, kb, 2 * half + tl, :],
                        rhs=bondsT[:, kb, :],
                        start=(kb == 0),
                        stop=(kb == BOND // P - 1),
                    )
            e_sums.append(e_ps)

        e_vwT = const.tile([P, PACK, TOKENS], F32)
        wcf_bias_all = const.tile([P, PACK, P], F32)
        wfc_bias = const.tile([P, P], F32)

        def finish_e_vw():
            wdf_bias = const.tile([P, PACK], F32)
            nc.vector.tensor_copy(out=wdf_bias[:], in_=wdf_bias_bf16[:])
            for t in range(PACK):
                nc.scalar.activation(
                    out=e_vwT[:, t, :], in_=e_sums[t // 2][:, t % 2, :], func=ACT.Identity, bias=wdf_bias[:, t : t + 1]
                )

        def spread_biases():
            bias_ps = bank_psum.tile([P, PACK, P], F32, tag="bank")
            for t in range(PACK):
                nc.tensor.matmul(
                    out=bias_ps[:, t, :],
                    lhsT=wcf_bias_bf16[:, t : t + 1].to_broadcast([P, P]),
                    rhs=ident_bf16[:],
                    start=True,
                    stop=True,
                )
            nc.vector.tensor_copy(out=wcf_bias_all[:], in_=bias_ps[:])
            wfc_bias_ps = bank_psum.tile([P, P], BF16, tag="bank")
            nc.tensor.transpose(wfc_bias_ps[:], wfc_bias_rows[:], ident_bf16[:])
            nc.vector.tensor_copy(out=wfc_bias[:], in_=wfc_bias_ps[:])

        h_w = [acc_psum.tile([P, HIDDEN], F32, tag="acc", name="h_w%d" % i) for i in range(TOKEN_TILES)]

        def multiply_step(k):
            for g in range(STEP * k, STEP * (k + 1)):
                r, j = divmod(g, ROUND)
                codes, plane = quantised[k][g % STEP]
                for i in range(TOKEN_TILES):
                    nc.tensor.matmul_mx(
                        out=h_w[i][:],
                        lhsT=codes[:, P * i : P * (i + 1)].bitcast(FP8X4),
                        lhsT_scale=plane[:, P * i : P * (i + 1)],
                        rhs=wcf_pieces[r][:, j, :].bitcast(FP8X4),
                        rhs_scale=wcf_planes[4 * j : P, r, :],
                        start=(g == 0),
                        stop=(g == GROUPS - 1),
                    )

        for k in range(STEPS):
            if k + AHEAD < STEPS:
                grouped = transpose_step(k + AHEAD)
                if k + AHEAD + 1 < STEPS:
                    sort_step(k + AHEAD + 1)
                quantised.append([quantise(x) for x in grouped])
            if k == 1:
                finish_e_vw()
            multiply_step(k)
            if k == 3:
                spread_biases()

        for quad in range(4):
            nc.sync.dma_start(
                out=wfc_first[32 * quad : 32 * quad + 4, :].bitcast(I32),
                in_=Wfc_w_scales[0, 4 * quad : 4 * quad + 4, 0 : PLANE_TILES * P].bitcast(I32),
            )
        wfc_pieces = []
        for c in range(CHUNKS):
            if c == 1:
                for quad in range(4):
                    nc.sync.dma_start(
                        out=wfc_planes[32 * quad : 32 * quad + 16, :].bitcast(I32),
                        in_=Wfc_w_scales[0, 4 * quad : 4 * quad + 4, :].rearrange("q (j n) -> j q n", j=4).bitcast(I32),
                    )
            piece = stream.tile([P, CHUNK_TILES * P], U32, tag="piece", align_bytes=64)
            parts = [(0, CHUNK_TILES * P)] if c > 0 else [(0, FIRST_TILES * P), (FIRST_TILES * P, CHUNK_TILES * P)]
            for start, end in parts:
                nc.sync.dma_start(
                    out=piece[:, start:end].bitcast(I32),
                    in_=wfc_words[:, CHUNK_TILES * P * c + start : CHUNK_TILES * P * c + end],
                )
            wfc_pieces.append(piece)

        h_grouped = const.tile([P, TOKENS, PACK], BF16, align_bytes=64)
        h_codes = const.tile([P, TOKENS], U32, align_bytes=64)
        h_plane = const.tile([P, TOKENS], U8, align_bytes=64)
        biased = []
        for i in range(TOKEN_TILES):
            h_wb = const.tile([P, PACK, P], F32, name="h_wb%d" % i)
            for t in range(0, PACK, 2):
                nc.vector.tensor_tensor(
                    out=h_wb[:, t : t + 2, :],
                    in0=h_w[i][:].rearrange("p (j t) -> p t j", t=PACK)[:, t : t + 2, :],
                    in1=wcf_bias_all[:, t : t + 2, :],
                    op=ALU.add,
                )
            biased.append(h_wb)
        for i in range(TOKEN_TILES):
            tokens = slice(P * i, P * (i + 1))
            h_wT = bank_psum.tile([P, PACK, P], F32, tag="bank")
            for t in range(PACK):
                nc.tensor.transpose(h_wT[:, t, :], biased[i][:, t, :], ident_f32[:])
            nc.vector.tensor_tensor(
                out=h_grouped[:, tokens, :],
                in0=h_wT[:].rearrange("p t c -> p c t"),
                in1=e_vwT[:, :, tokens].rearrange("p t c -> p c t"),
                op=ALU.mult,
            )
        for i in range(TOKEN_TILES):
            tokens = slice(P * i, P * (i + 1))
            nc.vector.quantize_mx(
                out=h_codes[:, tokens].bitcast(FP8X4),
                scales=h_plane[:, tokens],
                in_=h_grouped[:, tokens, :].rearrange("p c t -> p (c t)"),
            )

        sums = const.tile([P, ATOM_TILES * NODES], F32)

        def store_block(b):
            sums_ps = bank_psum.tile([P, P], F32, tag="bank")
            nc.tensor.transpose(sums_ps[:], sums[:, P * b : P * (b + 1)], ident_f32[:])
            rows = store_pool.tile([P, P], F32)
            nc.vector.tensor_copy(out=rows[:], in_=sums_ps[:])
            nc.sync.dma_start(
                out=out[:, BLOCK_TILES * P * b : BLOCK_TILES * P * (b + 1)].rearrange("n (a p) -> a n p", p=P),
                in_=rows[:],
            )

        for a in range(ATOM_TILES):
            cols = slice(P * (a % CHUNK_TILES), P * (a % CHUNK_TILES + 1))
            plane_cols = slice(P * (a % PLANE_TILES), P * (a % PLANE_TILES + 1))
            z = bank_psum.tile([P, TOKENS], F32, tag="bank")
            nc.tensor.matmul_mx(
                out=z[:],
                lhsT=wfc_pieces[a // CHUNK_TILES][:, cols].bitcast(FP8X4),
                lhsT_scale=wfc_first[:, plane_cols]
                if a < PLANE_TILES
                else wfc_planes[4 * (a // PLANE_TILES) : P, plane_cols],
                rhs=h_codes[:].bitcast(FP8X4),
                rhs_scale=h_plane[:],
                start=True,
                stop=True,
            )
            if a % SUM_TILES == 0:
                tanh_z = tanh_pool.tile([P, SUM_TILES, TOKENS], F32)
            nc.scalar.activation(out=tanh_z[:, a % SUM_TILES, :], in_=z[:], func=ACT.Tanh, bias=wfc_bias[:, a : a + 1])
            width = SUM_TILES if a < ATOM_TILES - SUM_TILES else 1
            if (a + 1) % width == 0:
                nc.vector.tensor_reduce(
                    out=sums[:, NODES * (a + 1 - width) : NODES * (a + 1)],
                    in_=tanh_z[:, (a + 1 - width) % SUM_TILES : a % SUM_TILES + 1, :].rearrange(
                        "p a (n k) -> p (a n) k", k=DEG
                    ),
                    axis=AXIS.X,
                    op=ALU.add,
                )
            if a >= BLOCK_TILES and a % BLOCK_TILES == STORE_LAG:
                store_block(a // BLOCK_TILES - 1)
        store_block(ATOM_TILES // BLOCK_TILES - 1)
